import numpy as np
import ml_dtypes


def mxq(x, axis, fmt="e4m3"):
    dtype, down = {"e4m3": (ml_dtypes.float8_e4m3fn, 7), "e5m2": (ml_dtypes.float8_e5m2, 14)}[fmt]
    v = np.moveaxis(np.asarray(x, np.float32).astype(ml_dtypes.bfloat16).astype(np.float64), axis, -1)
    blocks = v.reshape(v.shape[:-1] + (-1, 32))
    amax = np.abs(blocks).max(-1, keepdims=True)
    byte = np.maximum(np.where(amax > 0, np.frexp(amax)[1] - 1 + 127, 0) - down, 1)
    scale = np.exp2(byte - 127.0)
    codes = (blocks / scale).astype(np.float32).astype(dtype).astype(np.float64)
    return np.moveaxis((codes * scale).reshape(v.shape), -1, axis)


WIDE = False


def mx_kscale(k):
    if not WIDE:
        return np.ones(k)
    levels = np.array([10, -10, 5, -5, 0])
    a = np.random.permutation(np.resize(levels, k // 512 * 4)).reshape(k // 512, 4)
    idx = np.arange(k)
    return np.exp2(a[idx // 512, idx % 128 // 32])


BF16 = ml_dtypes.bfloat16


def bf(x):
    return np.asarray(x, np.float32).astype(BF16)


def f64(x):
    return np.asarray(x).astype(np.float64)


B, D = 8192, 512
C = 8.0


def sigmoid(v):
    return 1.0 / (1.0 + np.exp(-v))


def softplus(v):
    return np.logaddexp(v, 0.0)


def setup_inputs():
    s = mx_kscale(D)
    xt = bf(np.random.standard_normal((B, D)) * s)
    ht_minus_1 = bf(np.random.standard_normal((B, D)) * s)
    Wa = bf(np.random.standard_normal((D, D)) / np.sqrt(D) / s[None, :])
    Wx = bf(np.random.standard_normal((D, D)) / np.sqrt(D) / s[None, :])
    ba = bf(np.random.standard_normal((1, D)) * 0.1)
    bx = bf(np.random.standard_normal((1, D)) * 0.1)
    Lambda = bf(np.random.uniform(-3.0, -1.0, (1, D)))
    return {"xt": xt, "ht_minus_1": ht_minus_1, "Wa": Wa, "Wx": Wx, "ba": ba, "bx": bx, "Lambda": Lambda}


def reference(xt, ht_minus_1, Wa, Wx, ba, bx, Lambda):
    x = f64(xt)
    xq = mxq(x, 1, "e4m3")
    rt = sigmoid((xq @ mxq(f64(Wa), 1, "e4m3").T) + f64(ba))
    it = sigmoid((xq @ mxq(f64(Wx), 1, "e4m3").T) + f64(bx))
    log_at = -(C * softplus(f64(Lambda))) * rt
    at = np.exp(log_at)
    ht = at * f64(ht_minus_1) + np.sqrt(1.0 - at ** 2) * (it * x)
    return ht

@@ -1,0 +1,283 @@
+from contextlib import ExitStack
+
+import concourse.mybir as mybir
+from concourse.masks import make_identity
+
+FLOPS = 2 * 2 * 8192 * 512 * 512
+
+F32 = mybir.dt.float32
+BF16 = mybir.dt.bfloat16
+U32 = mybir.dt.uint32
+U8 = mybir.dt.uint8
+FP8X4 = mybir.dt.float8_e4m3fn_x4
+ACT = mybir.ActivationFunctionType
+ALU = mybir.AluOpType
+
+P = 128
+D = 512
+GB = 512
+NG = 16
+W4 = 4 * GB
+CHUNKS = (4, 4, 4, 4)
+NT = 4
+LX = 3
+LH = 2
+TAIL_V = ()
+
+
+def tile_cell_t_kernel(tc, xt, ht_minus_1, Wa, Wx, ba, bx, Lambda, out):
+    nc = tc.nc
+    x_v = xt.rearrange("(g p j) k -> g p (j k)", p=P, j=4)
+    h_v = ht_minus_1.rearrange("(g p j) k -> g p (j k)", p=P, j=4)
+    o_v = out.rearrange("(g p j) k -> g p (j k)", p=P, j=4)
+
+    with ExitStack() as ctx:
+        const = ctx.enter_context(tc.tile_pool(name="const", bufs=1))
+        xpool = ctx.enter_context(tc.tile_pool(name="xpool", bufs=max(CHUNKS) + LX))
+        hpool = ctx.enter_context(tc.tile_pool(name="hpool", bufs=4))
+        gpool = ctx.enter_context(tc.tile_pool(name="gpool", bufs=2))
+        cpool = ctx.enter_context(tc.tile_pool(name="cpool", bufs=3))
+        tapool = ctx.enter_context(tc.tile_pool(name="tapool", bufs=1))
+        ppool = ctx.enter_context(tc.tile_pool(name="ppool", bufs=max(CHUNKS) + 1))
+        apool = ctx.enter_context(tc.tile_pool(name="apool", bufs=max(CHUNKS) + 1))
+        rpool = ctx.enter_context(tc.tile_pool(name="rpool", bufs=max(CHUNKS) + 1))
+        psum = ctx.enter_context(tc.psum_pool(name="psum", bufs=1))
+        ctx.enter_context(tc.manual_schedule())
+
+        tcount = [0]
+
+        def tbank():
+            i = tcount[0]
+            tcount[0] = i + 1
+            return psum.tile([P, 512], F32, tag="T%d" % (i % NT), name="T_%d" % i)
+
+        xs, hs, codes, scales, za, zx = {}, {}, {}, {}, {}, {}
+        tas, ps, a2s, rs = {}, {}, {}, {}
+
+        ident = const.tile([P, P], F32, name="ident")
+        make_identity(nc, ident[:])
+        vt = const.tile([P, P], F32, name="vt")
+        nc.vector.memset(vt[:], 0.0)
+        one = const.tile([P, 1], F32, name="one")
+        nc.vector.memset(one[:], 1.0)
+        quarter = const.tile([P, 1], F32, name="quarter")
+        nc.vector.memset(quarter[:], 0.25)
+        vt_bf = vt[:].bitcast(BF16)
+        for v, vec in enumerate((ba, bx, Lambda)):
+            nc.scalar.dma_start(out=vt_bf[2 * v:2 * v + 2, :],
+                                in_=vec.rearrange("o (u w) -> (o u) w", u=2))
+
+        def load_x(g):
+            t = xpool.tile([P, W4], BF16, tag="x", name="x%d" % g)
+            nc.sync.dma_start(out=t[:], in_=x_v[g])
+            xs[g] = t
+
+        def load_h(g):
+            t = hpool.tile([P, W4], BF16, tag="h", name="h%d" % g)
+            nc.sync.dma_start(out=t[:], in_=h_v[g])
+            hs[g] = t
+
+        def load_w(w, name, eng):
+            t = xpool.tile([P, W4], BF16, tag="x", name=name)
+            eng.dma_start(out=t[:].rearrange("m (u f) -> m u f", u=2),
+                          in_=w.rearrange("(u m e) k -> m u (e k)", u=2, e=2))
+            return t
+
+        load_x(0)
+        wa_sb = load_w(Wa, "wa_sb", nc.scalar)
+        wx_sb = load_w(Wx, "wx_sb", nc.sync)
+        load_x(1)
+        load_x(2)
+        load_h(0)
+        load_h(1)
+
+        def word_transposes(src):
+            sv = src[:].bitcast(F32)
+            banks = []
+            for half in range(2):
+                bank = tbank()
+                for jl in range(2):
+                    for u in range(2):
+                        col = (2 * half + jl) * 256 + u * 128
+                        nc.tensor.transpose(bank[:, u * 256 + jl * 128:u * 256 + jl * 128 + 128],
+                                            sv[:, col:col + 128], ident[:])
+                banks.append(bank)
+            return banks
+
+        def regroup(src, name):
+            banks = word_transposes(src)
+            grp = gpool.tile([P, 1024], F32, tag="grp", name="grp_" + name, align_bytes=64)
+            for half in range(2):
+                nc.vector.tensor_copy(
+                    out=grp[:, half * 512:(half + 1) * 512].rearrange("p (c u) -> p c u", u=2),
+                    in_=banks[half][:].rearrange("p (u c) -> p c u", u=2))
+            return grp
+
+        def quantise(grp, cod, sca):
+            nc.vector.quantize_mx(out=cod[:].bitcast(FP8X4), scales=sca[:],
+                                  in_=grp[:].bitcast(BF16))
+
+        grps = {}
+
+        def prep_x(g):
+            grps[g] = regroup(xs[g], "x%d" % g)
+
+        def quant_x(g):
+            codes[g] = cpool.tile([P, GB], U32, tag="cod", name="cod%d" % g, align_bytes=64)
+            scales[g] = cpool.tile([P, GB], U8, tag="sca", name="sca%d" % g, align_bytes=64)
+            quantise(grps[g], codes[g], scales[g])
+
+        cbank = tbank()
+        nc.tensor.transpose(cbank[:, 0:P], vt[:], ident[:])
+        raw = const.tile([P, 12], F32, name="raw")
+        nc.vector.tensor_copy(out=raw[:], in_=cbank[:].bitcast(BF16)[:, 0:12])
+        hb = const.tile([P, 8], F32, name="hb")
+        nc.vector.tensor_scalar_mul(out=hb[:], in0=raw[:, 0:8], scalar1=0.5)
+        lam = raw[:, 8:12]
+        sp_a = const.tile([P, 4], F32, name="sp_a")
+        nc.scalar.activation(out=sp_a[:], in_=lam, func=ACT.Abs)
+        sp_e = const.tile([P, 4], F32, name="sp_e")
+        nc.scalar.activation(out=sp_e[:], in_=sp_a[:], func=ACT.Exp, scale=-1.0)
+        sp_l = const.tile([P, 4], F32, name="sp_l")
+        nc.scalar.activation(out=sp_l[:], in_=sp_e[:], func=ACT.Ln, bias=one[:])
+        sp = const.tile([P, 4], F32, name="sp")
+        nc.vector.scalar_tensor_tensor(out=sp[:], in0=lam, scalar=0.0, in1=sp_l[:],
+                                       op0=ALU.max, op1=ALU.add)
+        nc4 = const.tile([P, 4], F32, name="nc4")
+        nc.vector.tensor_scalar_mul(out=nc4[:], in0=sp[:], scalar1=-4.0)
+
+        wcod, wsca = {}, {}
+        prep_x(0)
+        ga = regroup(wa_sb, "wa")
+        quant_x(0)
+        for nm, in_grp in (("a", ga),):
+            wcod[nm] = const.tile([P, D], U32, name="wcod" + nm, align_bytes=64)
+            wsca[nm] = const.tile([P, D], U8, name="wsca" + nm, align_bytes=64)
+            quantise(in_grp, wcod[nm], wsca[nm])
+        gx = regroup(wx_sb, "wx")
+        prep_x(1)
+        wcod["x"] = const.tile([P, D], U32, name="wcodx", align_bytes=64)
+        wsca["x"] = const.tile([P, D], U8, name="wscax", align_bytes=64)
+        quantise(gx, wcod["x"], wsca["x"])
+        quant_x(1)
+
+        def mx(g, gate, store):
+            store[g] = []
+            for blk in range(4):
+                z = psum.tile([P, 512], F32, tag="Z%d" % blk, name="z%s%d_%d" % (gate, g, blk))
+                nc.tensor.matmul_mx(
+                    out=z[:],
+                    lhsT=wcod[gate][:, blk * P:(blk + 1) * P].bitcast(FP8X4),
+                    lhsT_scale=wsca[gate][:, blk * P:(blk + 1) * P],
+                    rhs=codes[g][:].bitcast(FP8X4),
+                    rhs_scale=scales[g][:],
+                    start=True, stop=True)
+                store[g].append(z)
+
+        def act_a(g):
+            tas[g] = tapool.tile([P, W4], F32, tag="ta", name="ta%d" % g)
+            for blk in range(4):
+                nc.scalar.activation(out=tas[g][:, blk * GB:(blk + 1) * GB], in_=za[g][blk][:],
+                                     func=ACT.Tanh, scale=0.5, bias=hb[:, blk:blk + 1])
+
+        def act_b(g):
+            ps[g] = ppool.tile([P, W4], F32, tag="p", name="p%d" % g)
+            for blk in range(4):
+                nc.scalar.activation(out=ps[g][:, blk * GB:(blk + 1) * GB], in_=zx[g][blk][:],
+                                     func=ACT.Tanh, scale=0.5, bias=hb[:, 4 + blk:5 + blk])
+
+        def act_c(g):
+            a2s[g] = apool.tile([P, W4], F32, tag="a2", name="a2_%d" % g)
+            for blk in range(4):
+                nc.scalar.activation(out=a2s[g][:, blk * GB:(blk + 1) * GB],
+                                     in_=tas[g][:, blk * GB:(blk + 1) * GB],
+                                     func=ACT.Exp, scale=nc4[:, blk:blk + 1], bias=nc4[:, blk:blk + 1])
+
+        def back_transposes(src, jj):
+            bank = tbank()
+            for blk in range(4):
+                nc.tensor.transpose(bank[:, blk * P:(blk + 1) * P],
+                                    src[:, blk * GB + jj * P:blk * GB + (jj + 1) * P], ident[:])
+            return bank[:].rearrange("p (u e m) -> p u m e", u=2, e=2)
+
+        def nat(t, jj):
+            return t[:, jj * D:(jj + 1) * D].rearrange("p (u m e) -> p u m e", u=2, e=2)
+
+        def at_h(g):
+            rs[g] = rpool.tile([P, W4], F32, tag="r", name="r%d" % g)
+            for jj in range(4):
+                bv = back_transposes(a2s[g], jj)
+                nc.vector.tensor_tensor(out=nat(rs[g], jj), in0=bv, in1=nat(hs[g], jj), op=ALU.mult)
+
+        def square(g):
+            nc.gpsimd.tensor_tensor(out=a2s[g][:], in0=a2s[g][:], in1=a2s[g][:], op=ALU.mult)
+
+        def act_e(g):
+            nc.scalar.activation(out=a2s[g][:], in_=a2s[g][:], func=ACT.Sqrt, scale=-0.25,
+                                 bias=quarter[:])
+
+        def fmul(g):
+            banks = word_transposes(xs[g])
+            pv = ps[g][:].rearrange("p (k n) -> p k n", k=4)
+            for half in range(2):
+                bv = banks[half][:].bitcast(BF16)
+                for u in range(2):
+                    io = pv[:, 2 * u:2 * u + 2, half * 256:(half + 1) * 256]
+                    nc.vector.scalar_tensor_tensor(
+                        out=io, in0=io, scalar=1.0,
+                        in1=bv[:, u * 512:(u + 1) * 512].rearrange("p (c e) -> p e c", e=2),
+                        op0=ALU.add, op1=ALU.mult)
+
+        def gmul(g):
+            eng = nc.vector if g in TAIL_V else nc.gpsimd
+            eng.tensor_tensor(out=ps[g][:], in0=ps[g][:], in1=a2s[g][:], op=ALU.mult)
+
+        def finish(g):
+            for jj in range(4):
+                bv = back_transposes(ps[g], jj)
+                nc.vector.tensor_tensor(out=nat(rs[g], jj), in0=bv, in1=nat(rs[g], jj), op=ALU.add)
+
+        def store(g):
+            nc.sync.dma_start(out=o_v[g], in_=rs[g][:])
+
+        mx(0, "a", za)
+        pending = []
+        g0 = 0
+        for n in CHUNKS:
+            chunk = list(range(g0, g0 + n))
+            g0 += n
+            for j, g in enumerate(chunk):
+                npop = -(-len(pending) // (n - j))
+                done = pending[:npop]
+                pending = pending[npop:]
+                for pg in done:
+                    finish(pg)
+                act_a(g)
+                mx(g, "x", zx)
+                act_b(g)
+                act_c(g)
+                if g + 2 < NG:
+                    prep_x(g + 2)
+                if j > 0:
+                    at_h(g - 1)
+                    square(g - 1)
+                if g + 2 < NG:
+                    quant_x(g + 2)
+                if g + 1 < NG:
+                    mx(g + 1, "a", za)
+                if g + LX < NG:
+                    load_x(g + LX)
+                if g + LH < NG:
+                    load_h(g + LH)
+                for pg in done:
+                    store(pg)
+            at_h(chunk[-1])
+            square(chunk[-1])
+            for g in chunk:
+                act_e(g)
+                fmul(g)
+                gmul(g)
+            pending = pending + chunk
+        for pg in pending:
+            finish(pg)
+            store(pg)

@@ -22,7 +22,6 @@ CHUNKS = (4, 4, 4, 4)
 NT = 4
 LX = 3
 LH = 2
-TAIL_V = ()
 
 
 def tile_cell_t_kernel(tc, xt, ht_minus_1, Wa, Wx, ba, bx, Lambda, out):
@@ -51,7 +50,7 @@ def tile_cell_t_kernel(tc, xt, ht_minus_1, Wa, Wx, ba, bx, Lambda, out):
             tcount[0] = i + 1
             return psum.tile([P, 512], F32, tag="T%d" % (i % NT), name="T_%d" % i)
 
-        xs, hs, codes, scales, za, zx = {}, {}, {}, {}, {}, {}
+        xs, hs, grps, codes, scales, zs = {}, {}, {}, {}, {}, {}
         tas, ps, a2s, rs = {}, {}, {}, {}
 
         ident = const.tile([P, P], F32, name="ident")
@@ -68,59 +67,55 @@ def tile_cell_t_kernel(tc, xt, ht_minus_1, Wa, Wx, ba, bx, Lambda, out):
                                 in_=vec.rearrange("o (u w) -> (o u) w", u=2))
 
         def load_x(g):
-            t = xpool.tile([P, W4], BF16, tag="x", name="x%d" % g)
-            nc.sync.dma_start(out=t[:], in_=x_v[g])
-            xs[g] = t
+            xs[g] = xpool.tile([P, W4], BF16, tag="x", name="x%d" % g)
+            nc.sync.dma_start(out=xs[g][:], in_=x_v[g])
 
         def load_h(g):
-            t = hpool.tile([P, W4], BF16, tag="h", name="h%d" % g)
-            nc.sync.dma_start(out=t[:], in_=h_v[g])
-            hs[g] = t
+            hs[g] = hpool.tile([P, W4], BF16, tag="h", name="h%d" % g)
+            nc.sync.dma_start(out=hs[g][:], in_=h_v[g])
 
-        def load_w(w, name, eng):
-            t = xpool.tile([P, W4], BF16, tag="x", name=name)
-            eng.dma_start(out=t[:].rearrange("m (u f) -> m u f", u=2),
-                          in_=w.rearrange("(u m e) k -> m u (e k)", u=2, e=2))
+        def load_w(u, eng):
+            t = xpool.tile([P, W4], BF16, tag="x", name="w_sb%d" % u)
+            for i, w in enumerate((Wa, Wx)):
+                eng.dma_start(out=t[:, i * 1024:(i + 1) * 1024],
+                              in_=w[256 * u:256 * (u + 1), :].rearrange("(m e) k -> m (e k)", e=2))
             return t
 
         load_x(0)
-        wa_sb = load_w(Wa, "wa_sb", nc.scalar)
-        wx_sb = load_w(Wx, "wx_sb", nc.sync)
+        w_sb = [load_w(0, nc.scalar)]
+        w_sb.append(load_w(1, nc.sync))
         load_x(1)
         load_x(2)
         load_h(0)
         load_h(1)
 
-        def word_transposes(src):
+        def word_transposes(src, half):
             sv = src[:].bitcast(F32)
-            banks = []
-            for half in range(2):
-                bank = tbank()
-                for jl in range(2):
-                    for u in range(2):
-                        col = (2 * half + jl) * 256 + u * 128
-                        nc.tensor.transpose(bank[:, u * 256 + jl * 128:u * 256 + jl * 128 + 128],
-                                            sv[:, col:col + 128], ident[:])
-                banks.append(bank)
-            return banks
+            bank = tbank()
+            for jl in range(2):
+                for u in range(2):
+                    col = (2 * half + jl) * 256 + u * 128
+                    nc.tensor.transpose(bank[:, u * 256 + jl * 128:u * 256 + jl * 128 + 128],
+                                        sv[:, col:col + 128], ident[:])
+            return bank
 
-        def regroup(src, name):
-            banks = word_transposes(src)
-            grp = gpool.tile([P, 1024], F32, tag="grp", name="grp_" + name, align_bytes=64)
-            for half in range(2):
-                nc.vector.tensor_copy(
-                    out=grp[:, half * 512:(half + 1) * 512].rearrange("p (c u) -> p c u", u=2),
-                    in_=banks[half][:].rearrange("p (u c) -> p c u", u=2))
-            return grp
+        def regroup_half(src, grp, half):
+            bank = word_transposes(src, half)
+            nc.vector.tensor_copy(
+                out=grp[:, half * 512:(half + 1) * 512].rearrange("p (c u) -> p c u", u=2),
+                in_=bank[:].rearrange("p (u c) -> p c u", u=2))
+
+        def new_grp(name):
+            return gpool.tile([P, 1024], F32, tag="grp", name="grp_" + name, align_bytes=64)
 
         def quantise(grp, cod, sca):
             nc.vector.quantize_mx(out=cod[:].bitcast(FP8X4), scales=sca[:],
                                   in_=grp[:].bitcast(BF16))
 
-        grps = {}
-
-        def prep_x(g):
-            grps[g] = regroup(xs[g], "x%d" % g)
+        def prep_x(g, half):
+            if half == 0:
+                grps[g] = new_grp("x%d" % g)
+            regroup_half(xs[g], grps[g], half)
 
         def quant_x(g):
             codes[g] = cpool.tile([P, GB], U32, tag="cod", name="cod%d" % g, align_bytes=64)
@@ -140,55 +135,53 @@ def tile_cell_t_kernel(tc, xt, ht_minus_1, Wa, Wx, ba, bx, Lambda, out):
         nc.scalar.activation(out=sp_e[:], in_=sp_a[:], func=ACT.Exp, scale=-1.0)
         sp_l = const.tile([P, 4], F32, name="sp_l")
         nc.scalar.activation(out=sp_l[:], in_=sp_e[:], func=ACT.Ln, bias=one[:])
-        sp = const.tile([P, 4], F32, name="sp")
-        nc.vector.scalar_tensor_tensor(out=sp[:], in0=lam, scalar=0.0, in1=sp_l[:],
-                                       op0=ALU.max, op1=ALU.add)
-        nc4 = const.tile([P, 4], F32, name="nc4")
-        nc.vector.tensor_scalar_mul(out=nc4[:], in0=sp[:], scalar1=-4.0)
 
-        wcod, wsca = {}, {}
-        prep_x(0)
-        ga = regroup(wa_sb, "wa")
+        wcod, wsca, wgrp = [], [], []
+        for u in range(2):
+            wcod.append(const.tile([P, D], U32, name="wcod%d" % u, align_bytes=64))
+            wsca.append(const.tile([P, D], U8, name="wsca%d" % u, align_bytes=64))
+        prep_x(0, 0)
+        prep_x(0, 1)
+        wgrp.append(new_grp("w0"))
+        regroup_half(w_sb[0], wgrp[0], 0)
+        regroup_half(w_sb[0], wgrp[0], 1)
         quant_x(0)
-        for nm, in_grp in (("a", ga),):
-            wcod[nm] = const.tile([P, D], U32, name="wcod" + nm, align_bytes=64)
-            wsca[nm] = const.tile([P, D], U8, name="wsca" + nm, align_bytes=64)
-            quantise(in_grp, wcod[nm], wsca[nm])
-        gx = regroup(wx_sb, "wx")
-        prep_x(1)
-        wcod["x"] = const.tile([P, D], U32, name="wcodx", align_bytes=64)
-        wsca["x"] = const.tile([P, D], U8, name="wscax", align_bytes=64)
-        quantise(gx, wcod["x"], wsca["x"])
-        quant_x(1)
+        quantise(wgrp[0], wcod[0], wsca[0])
+        sp = const.tile([P, 4], F32, name="sp")
+        nc4 = const.tile([P, 4], F32, name="nc4")
 
-        def mx(g, gate, store):
-            store[g] = []
-            for blk in range(4):
-                z = psum.tile([P, 512], F32, tag="Z%d" % blk, name="z%s%d_%d" % (gate, g, blk))
+        def mx(g, gate, u):
+            for e in range(2):
+                col = (2 * gate + e) * P
+                z = psum.tile([P, 512], F32, tag="Z%d" % (2 * gate + e),
+                              name="z%d_%d_%d" % (gate, g, 2 * u + e))
                 nc.tensor.matmul_mx(
                     out=z[:],
-                    lhsT=wcod[gate][:, blk * P:(blk + 1) * P].bitcast(FP8X4),
-                    lhsT_scale=wsca[gate][:, blk * P:(blk + 1) * P],
+                    lhsT=wcod[u][:, col:col + P].bitcast(FP8X4),
+                    lhsT_scale=wsca[u][:, col:col + P],
                     rhs=codes[g][:].bitcast(FP8X4),
                     rhs_scale=scales[g][:],
                     start=True, stop=True)
-                store[g].append(z)
+                zs[(g, gate, 2 * u + e)] = z
 
-        def act_a(g):
-            tas[g] = tapool.tile([P, W4], F32, tag="ta", name="ta%d" % g)
-            for blk in range(4):
-                nc.scalar.activation(out=tas[g][:, blk * GB:(blk + 1) * GB], in_=za[g][blk][:],
+        def act_a(g, u):
+            if u == 0:
+                tas[g] = tapool.tile([P, W4], F32, tag="ta", name="ta%d" % g)
+            for blk in (2 * u, 2 * u + 1):
+                nc.scalar.activation(out=tas[g][:, blk * GB:(blk + 1) * GB], in_=zs[(g, 0, blk)][:],
                                      func=ACT.Tanh, scale=0.5, bias=hb[:, blk:blk + 1])
 
-        def act_b(g):
-            ps[g] = ppool.tile([P, W4], F32, tag="p", name="p%d" % g)
-            for blk in range(4):
-                nc.scalar.activation(out=ps[g][:, blk * GB:(blk + 1) * GB], in_=zx[g][blk][:],
+        def act_b(g, u):
+            if u == 0:
+                ps[g] = ppool.tile([P, W4], F32, tag="p", name="p%d" % g)
+            for blk in (2 * u, 2 * u + 1):
+                nc.scalar.activation(out=ps[g][:, blk * GB:(blk + 1) * GB], in_=zs[(g, 1, blk)][:],
                                      func=ACT.Tanh, scale=0.5, bias=hb[:, 4 + blk:5 + blk])
 
-        def act_c(g):
-            a2s[g] = apool.tile([P, W4], F32, tag="a2", name="a2_%d" % g)
-            for blk in range(4):
+        def act_c(g, u):
+            if u == 0:
+                a2s[g] = apool.tile([P, W4], F32, tag="a2", name="a2_%d" % g)
+            for blk in (2 * u, 2 * u + 1):
                 nc.scalar.activation(out=a2s[g][:, blk * GB:(blk + 1) * GB],
                                      in_=tas[g][:, blk * GB:(blk + 1) * GB],
                                      func=ACT.Exp, scale=nc4[:, blk:blk + 1], bias=nc4[:, blk:blk + 1])
@@ -203,11 +196,11 @@ def tile_cell_t_kernel(tc, xt, ht_minus_1, Wa, Wx, ba, bx, Lambda, out):
         def nat(t, jj):
             return t[:, jj * D:(jj + 1) * D].rearrange("p (u m e) -> p u m e", u=2, e=2)
 
-        def at_h(g):
-            rs[g] = rpool.tile([P, W4], F32, tag="r", name="r%d" % g)
-            for jj in range(4):
-                bv = back_transposes(a2s[g], jj)
-                nc.vector.tensor_tensor(out=nat(rs[g], jj), in0=bv, in1=nat(hs[g], jj), op=ALU.mult)
+        def at_h(g, jj):
+            if jj == 0:
+                rs[g] = rpool.tile([P, W4], F32, tag="r", name="r%d" % g)
+            bv = back_transposes(a2s[g], jj)
+            nc.vector.tensor_tensor(out=nat(rs[g], jj), in0=bv, in1=nat(hs[g], jj), op=ALU.mult)
 
         def square(g):
             nc.gpsimd.tensor_tensor(out=a2s[g][:], in0=a2s[g][:], in1=a2s[g][:], op=ALU.mult)
@@ -217,10 +210,9 @@ def tile_cell_t_kernel(tc, xt, ht_minus_1, Wa, Wx, ba, bx, Lambda, out):
                                  bias=quarter[:])
 
         def fmul(g):
-            banks = word_transposes(xs[g])
             pv = ps[g][:].rearrange("p (k n) -> p k n", k=4)
             for half in range(2):
-                bv = banks[half][:].bitcast(BF16)
+                bv = word_transposes(xs[g], half)[:].bitcast(BF16)
                 for u in range(2):
                     io = pv[:, 2 * u:2 * u + 2, half * 256:(half + 1) * 256]
                     nc.vector.scalar_tensor_tensor(
@@ -229,55 +221,85 @@ def tile_cell_t_kernel(tc, xt, ht_minus_1, Wa, Wx, ba, bx, Lambda, out):
                         op0=ALU.add, op1=ALU.mult)
 
         def gmul(g):
-            eng = nc.vector if g in TAIL_V else nc.gpsimd
-            eng.tensor_tensor(out=ps[g][:], in0=ps[g][:], in1=a2s[g][:], op=ALU.mult)
+            nc.gpsimd.tensor_tensor(out=ps[g][:], in0=ps[g][:], in1=a2s[g][:], op=ALU.mult)
 
-        def finish(g):
-            for jj in range(4):
-                bv = back_transposes(ps[g], jj)
-                nc.vector.tensor_tensor(out=nat(rs[g], jj), in0=bv, in1=nat(rs[g], jj), op=ALU.add)
+        def finish(g, jj):
+            bv = back_transposes(ps[g], jj)
+            nc.vector.tensor_tensor(out=nat(rs[g], jj), in0=bv, in1=nat(rs[g], jj), op=ALU.add)
 
         def store(g):
             nc.sync.dma_start(out=o_v[g], in_=rs[g][:])
 
-        mx(0, "a", za)
+        mx(0, 0, 0)
+        mx(0, 1, 0)
+        wgrp.append(new_grp("w1"))
+        regroup_half(w_sb[1], wgrp[1], 0)
+        regroup_half(w_sb[1], wgrp[1], 1)
+        nc.vector.scalar_tensor_tensor(out=sp[:], in0=lam, scalar=0.0, in1=sp_l[:],
+                                       op0=ALU.max, op1=ALU.add)
+        nc.vector.tensor_scalar_mul(out=nc4[:], in0=sp[:], scalar1=-4.0)
+        prep_x(1, 0)
+        quantise(wgrp[1], wcod[1], wsca[1])
+        prep_x(1, 1)
         pending = []
         g0 = 0
         for n in CHUNKS:
             chunk = list(range(g0, g0 + n))
             g0 += n
             for j, g in enumerate(chunk):
-                npop = -(-len(pending) // (n - j))
-                done = pending[:npop]
-                pending = pending[npop:]
-                for pg in done:
-                    finish(pg)
-                act_a(g)
-                mx(g, "x", zx)
-                act_b(g)
-                act_c(g)
-                if g + 2 < NG:
-                    prep_x(g + 2)
+                pg = pending[0] if pending else None
+                pending = pending[1:]
+                more_x = g + 2 < NG
+                act_a(g, 0)
+                act_b(g, 0)
+                mx(g, 0, 1)
                 if j > 0:
-                    at_h(g - 1)
+                    at_h(g - 1, 0)
+                mx(g, 1, 1)
+                act_c(g, 0)
+                act_a(g, 1)
+                act_b(g, 1)
+                if g == 0:
+                    quant_x(1)
+                if j > 0:
+                    for jj in (1, 2, 3):
+                        at_h(g - 1, jj)
                     square(g - 1)
-                if g + 2 < NG:
+                if more_x:
+                    prep_x(g + 2, 0)
+                if j < n - 1:
+                    mx(g + 1, 0, 0)
+                if more_x:
+                    prep_x(g + 2, 1)
+                if j < n - 1:
+                    mx(g + 1, 1, 0)
+                act_c(g, 1)
+                if pg is not None:
+                    finish(pg, 0)
+                if more_x:
                     quant_x(g + 2)
-                if g + 1 < NG:
-                    mx(g + 1, "a", za)
+                if pg is not None:
+                    for jj in (1, 2, 3):
+                        finish(pg, jj)
                 if g + LX < NG:
                     load_x(g + LX)
                 if g + LH < NG:
                     load_h(g + LH)
-                for pg in done:
+                if pg is not None:
                     store(pg)
-            at_h(chunk[-1])
-            square(chunk[-1])
+            last = chunk[-1]
+            for jj in range(4):
+                at_h(last, jj)
+            square(last)
             for g in chunk:
                 act_e(g)
                 fmul(g)
                 gmul(g)
+            if last + 1 < NG:
+                mx(last + 1, 0, 0)
+                mx(last + 1, 1, 0)
             pending = pending + chunk
         for pg in pending:
-            finish(pg)
+            for jj in range(4):
+                finish(pg, jj)
             store(pg)

@@ -22,6 +22,7 @@ CHUNKS = (4, 4, 4, 4)
 NT = 4
 LX = 3
 LH = 2
+EARLY_F = {14: 12, 15: 13}
 
 
 def tile_cell_t_kernel(tc, xt, ht_minus_1, Wa, Wx, ba, bx, Lambda, out):
@@ -29,6 +30,7 @@ def tile_cell_t_kernel(tc, xt, ht_minus_1, Wa, Wx, ba, bx, Lambda, out):
     x_v = xt.rearrange("(g p j) k -> g p (j k)", p=P, j=4)
     h_v = ht_minus_1.rearrange("(g p j) k -> g p (j k)", p=P, j=4)
     o_v = out.rearrange("(g p j) k -> g p (j k)", p=P, j=4)
+    o_v4 = out.rearrange("(g p j) k -> g p j k", p=P, j=4)
 
     with ExitStack() as ctx:
         const = ctx.enter_context(tc.tile_pool(name="const", bufs=1))
@@ -209,19 +211,29 @@ def tile_cell_t_kernel(tc, xt, ht_minus_1, Wa, Wx, ba, bx, Lambda, out):
             nc.scalar.activation(out=a2s[g][:], in_=a2s[g][:], func=ACT.Sqrt, scale=-0.25,
                                  bias=quarter[:])
 
-        def fmul(g):
+        def fmul(g, half):
             pv = ps[g][:].rearrange("p (k n) -> p k n", k=4)
-            for half in range(2):
-                bv = word_transposes(xs[g], half)[:].bitcast(BF16)
-                for u in range(2):
-                    io = pv[:, 2 * u:2 * u + 2, half * 256:(half + 1) * 256]
-                    nc.vector.scalar_tensor_tensor(
-                        out=io, in0=io, scalar=1.0,
-                        in1=bv[:, u * 512:(u + 1) * 512].rearrange("p (c e) -> p e c", e=2),
-                        op0=ALU.add, op1=ALU.mult)
+            bv = word_transposes(xs[g], half)[:].bitcast(BF16)
+            for u in range(2):
+                io = pv[:, 2 * u:2 * u + 2, half * 256:(half + 1) * 256]
+                nc.vector.scalar_tensor_tensor(
+                    out=io, in0=io, scalar=1.0,
+                    in1=bv[:, u * 512:(u + 1) * 512].rearrange("p (c e) -> p e c", e=2),
+                    op0=ALU.add, op1=ALU.mult)
 
         def gmul(g):
             nc.gpsimd.tensor_tensor(out=ps[g][:], in0=ps[g][:], in1=a2s[g][:], op=ALU.mult)
+
+        def gmul_quarter(g, jj, eng):
+            pv = ps[g][:].rearrange("p (k n) -> p k n", k=4)[:, :, jj * P:(jj + 1) * P]
+            sv = a2s[g][:].rearrange("p (k n) -> p k n", k=4)[:, :, jj * P:(jj + 1) * P]
+            eng.tensor_tensor(out=pv, in0=pv, in1=sv, op=ALU.mult)
+
+        def square_on_scalar(g):
+            nc.scalar.activation(out=a2s[g][:], in_=a2s[g][:], func=ACT.Square)
+
+        def store_quarter(g, jj):
+            nc.sync.dma_start(out=o_v4[g][:, jj, :], in_=rs[g][:, jj * D:(jj + 1) * D])
 
         def finish(g, jj):
             bv = back_transposes(ps[g], jj)
@@ -243,44 +255,63 @@ def tile_cell_t_kernel(tc, xt, ht_minus_1, Wa, Wx, ba, bx, Lambda, out):
         prep_x(1, 1)
         pending = []
         g0 = 0
-        for n in CHUNKS:
+        for ci, n in enumerate(CHUNKS):
             chunk = list(range(g0, g0 + n))
             g0 += n
+            last_chunk = ci == len(CHUNKS) - 1
             for j, g in enumerate(chunk):
                 pg = pending[0] if pending else None
                 pending = pending[1:]
                 more_x = g + 2 < NG
+                banks = []
+                if j > 0:
+                    banks.extend([("R", g - 1, jj) for jj in range(4)])
+                if more_x:
+                    banks.extend([("K", g + 2, 0), ("K", g + 2, 1)])
+                if pg is not None:
+                    banks.extend([("O", pg, jj) for jj in range(4)])
+                if g in EARLY_F:
+                    banks.extend([("F", EARLY_F[g], 0), ("F", EARLY_F[g], 1)])
+                state = {"i": 0, "quant": not more_x}
+
+                def emit(count):
+                    for item in banks[state["i"]:state["i"] + count]:
+                        kind, gg, part = item
+                        if kind == "R":
+                            at_h(gg, part)
+                            if part == 3:
+                                square(gg)
+                        elif kind == "K":
+                            prep_x(gg, part)
+                        elif kind == "F":
+                            fmul(gg, part)
+                        else:
+                            finish(gg, part)
+                            if not state["quant"]:
+                                quant_x(g + 2)
+                                state["quant"] = True
+                    state["i"] = state["i"] + count
+
                 act_a(g, 0)
                 act_b(g, 0)
                 mx(g, 0, 1)
-                if j > 0:
-                    at_h(g - 1, 0)
+                emit(1)
                 mx(g, 1, 1)
                 act_c(g, 0)
                 act_a(g, 1)
                 act_b(g, 1)
                 if g == 0:
                     quant_x(1)
-                if j > 0:
-                    for jj in (1, 2, 3):
-                        at_h(g - 1, jj)
-                    square(g - 1)
-                if more_x:
-                    prep_x(g + 2, 0)
+                emit(4)
                 if j < n - 1:
                     mx(g + 1, 0, 0)
-                if more_x:
-                    prep_x(g + 2, 1)
+                emit(1)
                 if j < n - 1:
                     mx(g + 1, 1, 0)
                 act_c(g, 1)
-                if pg is not None:
-                    finish(pg, 0)
-                if more_x:
+                emit(len(banks))
+                if not state["quant"]:
                     quant_x(g + 2)
-                if pg is not None:
-                    for jj in (1, 2, 3):
-                        finish(pg, jj)
                 if g + LX < NG:
                     load_x(g + LX)
                 if g + LH < NG:
@@ -288,18 +319,32 @@ def tile_cell_t_kernel(tc, xt, ht_minus_1, Wa, Wx, ba, bx, Lambda, out):
                 if pg is not None:
                     store(pg)
             last = chunk[-1]
-            for jj in range(4):
-                at_h(last, jj)
-            square(last)
-            for g in chunk:
-                act_e(g)
-                fmul(g)
-                gmul(g)
-            if last + 1 < NG:
+            early = [EARLY_F[k] for k in EARLY_F]
+            if last_chunk:
+                for jj in range(4):
+                    at_h(last, jj)
+                for g in chunk:
+                    if g == last:
+                        square_on_scalar(g)
+                    act_e(g)
+                    if g not in early:
+                        fmul(g, 0)
+                        fmul(g, 1)
+                    for jj in range(4):
+                        gmul_quarter(g, jj, nc.vector if jj == 3 else nc.gpsimd)
+            else:
+                for jj in range(4):
+                    at_h(last, jj)
+                square(last)
+                for g in chunk:
+                    act_e(g)
+                    fmul(g, 0)
+                    fmul(g, 1)
+                    gmul(g)
                 mx(last + 1, 0, 0)
                 mx(last + 1, 1, 0)
             pending = pending + chunk
         for pg in pending:
             for jj in range(4):
                 finish(pg, jj)
-            store(pg)
+                store_quarter(pg, jj)

@@ -22,6 +22,7 @@ CHUNKS = (4, 4, 4, 4)
 NT = 4
 LX = 3
 LH = 2
+MX_POS = 2
 EARLY_F = {14: 12, 15: 13}
 
 
@@ -229,6 +230,13 @@ def tile_cell_t_kernel(tc, xt, ht_minus_1, Wa, Wx, ba, bx, Lambda, out):
             sv = a2s[g][:].rearrange("p (k n) -> p k n", k=4)[:, :, jj * P:(jj + 1) * P]
             eng.tensor_tensor(out=pv, in0=pv, in1=sv, op=ALU.mult)
 
+        def square_aside(g):
+            nc.gpsimd.tensor_tensor(out=tas[g][:], in0=a2s[g][:], in1=a2s[g][:], op=ALU.mult)
+
+        def act_e_aside(g):
+            nc.scalar.activation(out=a2s[g][:], in_=tas[g][:], func=ACT.Sqrt, scale=-0.25,
+                                 bias=quarter[:])
+
         def square_on_scalar(g):
             nc.scalar.activation(out=a2s[g][:], in_=a2s[g][:], func=ACT.Square)
 
@@ -250,8 +258,8 @@ def tile_cell_t_kernel(tc, xt, ht_minus_1, Wa, Wx, ba, bx, Lambda, out):
         nc.vector.scalar_tensor_tensor(out=sp[:], in0=lam, scalar=0.0, in1=sp_l[:],
                                        op0=ALU.max, op1=ALU.add)
         nc.vector.tensor_scalar_mul(out=nc4[:], in0=sp[:], scalar1=-4.0)
-        prep_x(1, 0)
         quantise(wgrp[1], wcod[1], wsca[1])
+        prep_x(1, 0)
         prep_x(1, 1)
         pending = []
         g0 = 0
@@ -331,18 +339,22 @@ def tile_cell_t_kernel(tc, xt, ht_minus_1, Wa, Wx, ba, bx, Lambda, out):
                         fmul(g, 0)
                         fmul(g, 1)
                     for jj in range(4):
-                        gmul_quarter(g, jj, nc.vector if jj == 3 else nc.gpsimd)
+                        gmul_quarter(g, jj, nc.gpsimd)
             else:
+                square_aside(last)
                 for jj in range(4):
                     at_h(last, jj)
-                square(last)
-                for g in chunk:
-                    act_e(g)
+                for i, g in enumerate(chunk):
+                    if i == MX_POS:
+                        mx(last + 1, 0, 0)
+                        mx(last + 1, 1, 0)
+                    if g == last:
+                        act_e_aside(g)
+                    else:
+                        act_e(g)
                     fmul(g, 0)
                     fmul(g, 1)
                     gmul(g)
-                mx(last + 1, 0, 0)
-                mx(last + 1, 1, 0)
             pending = pending + chunk
         for pg in pending:
             for jj in range(4):

@@ -40,7 +40,7 @@ def tile_cell_t_kernel(tc, xt, ht_minus_1, Wa, Wx, ba, bx, Lambda, out):
         gpool = ctx.enter_context(tc.tile_pool(name="gpool", bufs=2))
         cpool = ctx.enter_context(tc.tile_pool(name="cpool", bufs=3))
         tapool = ctx.enter_context(tc.tile_pool(name="tapool", bufs=1))
-        ppool = ctx.enter_context(tc.tile_pool(name="ppool", bufs=max(CHUNKS) + 1))
+        ppool = ctx.enter_context(tc.tile_pool(name="ppool", bufs=max(CHUNKS) + 2))
         apool = ctx.enter_context(tc.tile_pool(name="apool", bufs=max(CHUNKS) + 1))
         rpool = ctx.enter_context(tc.tile_pool(name="rpool", bufs=max(CHUNKS) + 1))
         psum = ctx.enter_context(tc.psum_pool(name="psum", bufs=1))
@@ -303,17 +303,17 @@ def tile_cell_t_kernel(tc, xt, ht_minus_1, Wa, Wx, ba, bx, Lambda, out):
                 act_a(g, 0)
                 act_b(g, 0)
                 mx(g, 0, 1)
-                emit(1)
+                emit(2)
                 mx(g, 1, 1)
                 act_c(g, 0)
                 act_a(g, 1)
                 act_b(g, 1)
                 if g == 0:
                     quant_x(1)
-                emit(4)
+                emit(3)
                 if j < n - 1:
                     mx(g + 1, 0, 0)
-                emit(1)
+                emit(2)
                 if j < n - 1:
                     mx(g + 1, 1, 0)
                 act_c(g, 1)

from contextlib import ExitStack

import concourse.mybir as mybir
from concourse.masks import make_identity

FLOPS = 2 * 2 * 8192 * 512 * 512

F32 = mybir.dt.float32
BF16 = mybir.dt.bfloat16
U32 = mybir.dt.uint32
U8 = mybir.dt.uint8
FP8X4 = mybir.dt.float8_e4m3fn_x4
ACT = mybir.ActivationFunctionType
ALU = mybir.AluOpType

P = 128
D = 512
GB = 512
NG = 16
W4 = 4 * GB
CHUNKS = (4, 4, 4, 4)
NT = 4
LX = 3
LH = 2
MX_POS = 2
EARLY_F = {14: 12, 15: 13}


def tile_cell_t_kernel(tc, xt, ht_minus_1, Wa, Wx, ba, bx, Lambda, out):
    nc = tc.nc
    x_v = xt.rearrange("(g p j) k -> g p (j k)", p=P, j=4)
    h_v = ht_minus_1.rearrange("(g p j) k -> g p (j k)", p=P, j=4)
    o_v = out.rearrange("(g p j) k -> g p (j k)", p=P, j=4)
    o_v4 = out.rearrange("(g p j) k -> g p j k", p=P, j=4)

    with ExitStack() as ctx:
        const = ctx.enter_context(tc.tile_pool(name="const", bufs=1))
        xpool = ctx.enter_context(tc.tile_pool(name="xpool", bufs=max(CHUNKS) + LX))
        hpool = ctx.enter_context(tc.tile_pool(name="hpool", bufs=4))
        gpool = ctx.enter_context(tc.tile_pool(name="gpool", bufs=2))
        cpool = ctx.enter_context(tc.tile_pool(name="cpool", bufs=3))
        tapool = ctx.enter_context(tc.tile_pool(name="tapool", bufs=1))
        ppool = ctx.enter_context(tc.tile_pool(name="ppool", bufs=max(CHUNKS) + 2))
        apool = ctx.enter_context(tc.tile_pool(name="apool", bufs=max(CHUNKS) + 1))
        rpool = ctx.enter_context(tc.tile_pool(name="rpool", bufs=max(CHUNKS) + 1))
        psum = ctx.enter_context(tc.psum_pool(name="psum", bufs=1))
        ctx.enter_context(tc.manual_schedule())

        tcount = [0]

        def tbank():
            i = tcount[0]
            tcount[0] = i + 1
            return psum.tile([P, 512], F32, tag="T%d" % (i % NT), name="T_%d" % i)

        xs, hs, grps, codes, scales, zs = {}, {}, {}, {}, {}, {}
        tas, ps, a2s, rs = {}, {}, {}, {}

        ident = const.tile([P, P], F32, name="ident")
        make_identity(nc, ident[:])
        vt = const.tile([P, P], F32, name="vt")
        nc.vector.memset(vt[:], 0.0)
        one = const.tile([P, 1], F32, name="one")
        nc.vector.memset(one[:], 1.0)
        quarter = const.tile([P, 1], F32, name="quarter")
        nc.vector.memset(quarter[:], 0.25)
        vt_bf = vt[:].bitcast(BF16)
        for v, vec in enumerate((ba, bx, Lambda)):
            nc.scalar.dma_start(out=vt_bf[2 * v:2 * v + 2, :],
                                in_=vec.rearrange("o (u w) -> (o u) w", u=2))

        def load_x(g):
            xs[g] = xpool.tile([P, W4], BF16, tag="x", name="x%d" % g)
            nc.sync.dma_start(out=xs[g][:], in_=x_v[g])

        def load_h(g):
            hs[g] = hpool.tile([P, W4], BF16, tag="h", name="h%d" % g)
            nc.sync.dma_start(out=hs[g][:], in_=h_v[g])

        def load_w(u, eng):
            t = xpool.tile([P, W4], BF16, tag="x", name="w_sb%d" % u)
            for i, w in enumerate((Wa, Wx)):
                eng.dma_start(out=t[:, i * 1024:(i + 1) * 1024],
                              in_=w[256 * u:256 * (u + 1), :].rearrange("(m e) k -> m (e k)", e=2))
            return t

        load_x(0)
        w_sb = [load_w(0, nc.scalar)]
        w_sb.append(load_w(1, nc.sync))
        load_x(1)
        load_x(2)
        load_h(0)
        load_h(1)

        def word_transposes(src, half):
            sv = src[:].bitcast(F32)
            bank = tbank()
            for jl in range(2):
                for u in range(2):
                    col = (2 * half + jl) * 256 + u * 128
                    nc.tensor.transpose(bank[:, u * 256 + jl * 128:u * 256 + jl * 128 + 128],
                                        sv[:, col:col + 128], ident[:])
            return bank

        def regroup_half(src, grp, half):
            bank = word_transposes(src, half)
            nc.vector.tensor_copy(
                out=grp[:, half * 512:(half + 1) * 512].rearrange("p (c u) -> p c u", u=2),
                in_=bank[:].rearrange("p (u c) -> p c u", u=2))

        def new_grp(name):
            return gpool.tile([P, 1024], F32, tag="grp", name="grp_" + name, align_bytes=64)

        def quantise(grp, cod, sca):
            nc.vector.quantize_mx(out=cod[:].bitcast(FP8X4), scales=sca[:],
                                  in_=grp[:].bitcast(BF16))

        def prep_x(g, half):
            if half == 0:
                grps[g] = new_grp("x%d" % g)
            regroup_half(xs[g], grps[g], half)

        def quant_x(g):
            codes[g] = cpool.tile([P, GB], U32, tag="cod", name="cod%d" % g, align_bytes=64)
            scales[g] = cpool.tile([P, GB], U8, tag="sca", name="sca%d" % g, align_bytes=64)
            quantise(grps[g], codes[g], scales[g])

        cbank = tbank()
        nc.tensor.transpose(cbank[:, 0:P], vt[:], ident[:])
        raw = const.tile([P, 12], F32, name="raw")
        nc.vector.tensor_copy(out=raw[:], in_=cbank[:].bitcast(BF16)[:, 0:12])
        hb = const.tile([P, 8], F32, name="hb")
        nc.vector.tensor_scalar_mul(out=hb[:], in0=raw[:, 0:8], scalar1=0.5)
        lam = raw[:, 8:12]
        sp_a = const.tile([P, 4], F32, name="sp_a")
        nc.scalar.activation(out=sp_a[:], in_=lam, func=ACT.Abs)
        sp_e = const.tile([P, 4], F32, name="sp_e")
        nc.scalar.activation(out=sp_e[:], in_=sp_a[:], func=ACT.Exp, scale=-1.0)
        sp_l = const.tile([P, 4], F32, name="sp_l")
        nc.scalar.activation(out=sp_l[:], in_=sp_e[:], func=ACT.Ln, bias=one[:])

        wcod, wsca, wgrp = [], [], []
        for u in range(2):
            wcod.append(const.tile([P, D], U32, name="wcod%d" % u, align_bytes=64))
            wsca.append(const.tile([P, D], U8, name="wsca%d" % u, align_bytes=64))
        prep_x(0, 0)
        prep_x(0, 1)
        wgrp.append(new_grp("w0"))
        regroup_half(w_sb[0], wgrp[0], 0)
        regroup_half(w_sb[0], wgrp[0], 1)
        quant_x(0)
        quantise(wgrp[0], wcod[0], wsca[0])
        sp = const.tile([P, 4], F32, name="sp")
        nc4 = const.tile([P, 4], F32, name="nc4")

        def mx(g, gate, u):
            for e in range(2):
                col = (2 * gate + e) * P
                z = psum.tile([P, 512], F32, tag="Z%d" % (2 * gate + e),
                              name="z%d_%d_%d" % (gate, g, 2 * u + e))
                nc.tensor.matmul_mx(
                    out=z[:],
                    lhsT=wcod[u][:, col:col + P].bitcast(FP8X4),
                    lhsT_scale=wsca[u][:, col:col + P],
                    rhs=codes[g][:].bitcast(FP8X4),
                    rhs_scale=scales[g][:],
                    start=True, stop=True)
                zs[(g, gate, 2 * u + e)] = z

        def act_a(g, u):
            if u == 0:
                tas[g] = tapool.tile([P, W4], F32, tag="ta", name="ta%d" % g)
            for blk in (2 * u, 2 * u + 1):
                nc.scalar.activation(out=tas[g][:, blk * GB:(blk + 1) * GB], in_=zs[(g, 0, blk)][:],
                                     func=ACT.Tanh, scale=0.5, bias=hb[:, blk:blk + 1])

        def act_b(g, u):
            if u == 0:
                ps[g] = ppool.tile([P, W4], F32, tag="p", name="p%d" % g)
            for blk in (2 * u, 2 * u + 1):
                nc.scalar.activation(out=ps[g][:, blk * GB:(blk + 1) * GB], in_=zs[(g, 1, blk)][:],
                                     func=ACT.Tanh, scale=0.5, bias=hb[:, 4 + blk:5 + blk])

        def act_c(g, u):
            if u == 0:
                a2s[g] = apool.tile([P, W4], F32, tag="a2", name="a2_%d" % g)
            for blk in (2 * u, 2 * u + 1):
                nc.scalar.activation(out=a2s[g][:, blk * GB:(blk + 1) * GB],
                                     in_=tas[g][:, blk * GB:(blk + 1) * GB],
                                     func=ACT.Exp, scale=nc4[:, blk:blk + 1], bias=nc4[:, blk:blk + 1])

        def back_transposes(src, jj):
            bank = tbank()
            for blk in range(4):
                nc.tensor.transpose(bank[:, blk * P:(blk + 1) * P],
                                    src[:, blk * GB + jj * P:blk * GB + (jj + 1) * P], ident[:])
            return bank[:].rearrange("p (u e m) -> p u m e", u=2, e=2)

        def nat(t, jj):
            return t[:, jj * D:(jj + 1) * D].rearrange("p (u m e) -> p u m e", u=2, e=2)

        def at_h(g, jj):
            if jj == 0:
                rs[g] = rpool.tile([P, W4], F32, tag="r", name="r%d" % g)
            bv = back_transposes(a2s[g], jj)
            nc.vector.tensor_tensor(out=nat(rs[g], jj), in0=bv, in1=nat(hs[g], jj), op=ALU.mult)

        def square(g):
            nc.gpsimd.tensor_tensor(out=a2s[g][:], in0=a2s[g][:], in1=a2s[g][:], op=ALU.mult)

        def act_e(g):
            nc.scalar.activation(out=a2s[g][:], in_=a2s[g][:], func=ACT.Sqrt, scale=-0.25,
                                 bias=quarter[:])

        def fmul(g, half):
            pv = ps[g][:].rearrange("p (k n) -> p k n", k=4)
            bv = word_transposes(xs[g], half)[:].bitcast(BF16)
            for u in range(2):
                io = pv[:, 2 * u:2 * u + 2, half * 256:(half + 1) * 256]
                nc.vector.scalar_tensor_tensor(
                    out=io, in0=io, scalar=1.0,
                    in1=bv[:, u * 512:(u + 1) * 512].rearrange("p (c e) -> p e c", e=2),
                    op0=ALU.add, op1=ALU.mult)

        def gmul(g):
            nc.gpsimd.tensor_tensor(out=ps[g][:], in0=ps[g][:], in1=a2s[g][:], op=ALU.mult)

        def gmul_quarter(g, jj, eng):
            pv = ps[g][:].rearrange("p (k n) -> p k n", k=4)[:, :, jj * P:(jj + 1) * P]
            sv = a2s[g][:].rearrange("p (k n) -> p k n", k=4)[:, :, jj * P:(jj + 1) * P]
            eng.tensor_tensor(out=pv, in0=pv, in1=sv, op=ALU.mult)

        def square_aside(g):
            nc.gpsimd.tensor_tensor(out=tas[g][:], in0=a2s[g][:], in1=a2s[g][:], op=ALU.mult)

        def act_e_aside(g):
            nc.scalar.activation(out=a2s[g][:], in_=tas[g][:], func=ACT.Sqrt, scale=-0.25,
                                 bias=quarter[:])

        def square_on_scalar(g):
            nc.scalar.activation(out=a2s[g][:], in_=a2s[g][:], func=ACT.Square)

        def store_quarter(g, jj):
            nc.sync.dma_start(out=o_v4[g][:, jj, :], in_=rs[g][:, jj * D:(jj + 1) * D])

        def finish(g, jj):
            bv = back_transposes(ps[g], jj)
            nc.vector.tensor_tensor(out=nat(rs[g], jj), in0=bv, in1=nat(rs[g], jj), op=ALU.add)

        def store(g):
            nc.sync.dma_start(out=o_v[g], in_=rs[g][:])

        mx(0, 0, 0)
        mx(0, 1, 0)
        wgrp.append(new_grp("w1"))
        regroup_half(w_sb[1], wgrp[1], 0)
        regroup_half(w_sb[1], wgrp[1], 1)
        nc.vector.scalar_tensor_tensor(out=sp[:], in0=lam, scalar=0.0, in1=sp_l[:],
                                       op0=ALU.max, op1=ALU.add)
        nc.vector.tensor_scalar_mul(out=nc4[:], in0=sp[:], scalar1=-4.0)
        quantise(wgrp[1], wcod[1], wsca[1])
        prep_x(1, 0)
        prep_x(1, 1)
        pending = []
        g0 = 0
        for ci, n in enumerate(CHUNKS):
            chunk = list(range(g0, g0 + n))
            g0 += n
            last_chunk = ci == len(CHUNKS) - 1
            for j, g in enumerate(chunk):
                pg = pending[0] if pending else None
                pending = pending[1:]
                more_x = g + 2 < NG
                banks = []
                if j > 0:
                    banks.extend([("R", g - 1, jj) for jj in range(4)])
                if more_x:
                    banks.extend([("K", g + 2, 0), ("K", g + 2, 1)])
                if pg is not None:
                    banks.extend([("O", pg, jj) for jj in range(4)])
                if g in EARLY_F:
                    banks.extend([("F", EARLY_F[g], 0), ("F", EARLY_F[g], 1)])
                state = {"i": 0, "quant": not more_x}

                def emit(count):
                    for item in banks[state["i"]:state["i"] + count]:
                        kind, gg, part = item
                        if kind == "R":
                            at_h(gg, part)
                            if part == 3:
                                square(gg)
                        elif kind == "K":
                            prep_x(gg, part)
                        elif kind == "F":
                            fmul(gg, part)
                        else:
                            finish(gg, part)
                            if not state["quant"]:
                                quant_x(g + 2)
                                state["quant"] = True
                    state["i"] = state["i"] + count

                act_a(g, 0)
                act_b(g, 0)
                mx(g, 0, 1)
                emit(2)
                mx(g, 1, 1)
                act_c(g, 0)
                act_a(g, 1)
                act_b(g, 1)
                if g == 0:
                    quant_x(1)
                emit(3)
                if j < n - 1:
                    mx(g + 1, 0, 0)
                emit(2)
                if j < n - 1:
                    mx(g + 1, 1, 0)
                act_c(g, 1)
                emit(len(banks))
                if not state["quant"]:
                    quant_x(g + 2)
                if g + LX < NG:
                    load_x(g + LX)
                if g + LH < NG:
                    load_h(g + LH)
                if pg is not None:
                    store(pg)
            last = chunk[-1]
            early = [EARLY_F[k] for k in EARLY_F]
            if last_chunk:
                for jj in range(4):
                    at_h(last, jj)
                for g in chunk:
                    if g == last:
                        square_on_scalar(g)
                    act_e(g)
                    if g not in early:
                        fmul(g, 0)
                        fmul(g, 1)
                    for jj in range(4):
                        gmul_quarter(g, jj, nc.gpsimd)
            else:
                square_aside(last)
                for jj in range(4):
                    at_h(last, jj)
                for i, g in enumerate(chunk):
                    if i == MX_POS:
                        mx(last + 1, 0, 0)
                        mx(last + 1, 1, 0)
                    if g == last:
                        act_e_aside(g)
                    else:
                        act_e(g)
                    fmul(g, 0)
                    fmul(g, 1)
                    gmul(g)
            pending = pending + chunk
        for pg in pending:
            for jj in range(4):
                finish(pg, jj)
                store_quarter(pg, jj)
